import numpy as np
import ml_dtypes


def mxq(x, axis, fmt="e4m3"):
    dtype, down = {"e4m3": (ml_dtypes.float8_e4m3fn, 7), "e5m2": (ml_dtypes.float8_e5m2, 14)}[fmt]
    v = np.moveaxis(np.asarray(x, np.float32).astype(ml_dtypes.bfloat16).astype(np.float64), axis, -1)
    blocks = v.reshape(v.shape[:-1] + (-1, 32))
    amax = np.abs(blocks).max(-1, keepdims=True)
    byte = np.maximum(np.where(amax > 0, np.frexp(amax)[1] - 1 + 127, 0) - down, 1)
    scale = np.exp2(byte - 127.0)
    codes = (blocks / scale).astype(np.float32).astype(dtype).astype(np.float64)
    return np.moveaxis((codes * scale).reshape(v.shape), -1, axis)


WIDE = False


def mx_kscale(k):
    if not WIDE:
        return np.ones(k)
    levels = np.array([10, -10, 5, -5, 0])
    a = np.random.permutation(np.resize(levels, k // 512 * 4)).reshape(k // 512, 4)
    idx = np.arange(k)
    return np.exp2(a[idx // 512, idx % 128 // 32])


BF16 = ml_dtypes.bfloat16


def bf(x):
    return np.asarray(x, np.float32).astype(BF16)


def f64(x):
    return np.asarray(x).astype(np.float64)


E2M1 = np.array([0.0, 0.5, 1.0, 1.5, 2.0, 3.0, 4.0, 6.0, -0.0, -0.5, -1.0, -1.5, -2.0, -3.0, -4.0, -6.0])


def pack_weight(w, fmt):
    k, n = w.shape
    w = f64(bf(w)).reshape(k // 32, 32, n)
    amax = np.abs(w).max(1)
    if fmt == "e4m3":
        byte = np.frexp(amax)[1] - 1 + 127 - 7
    else:
        mant, ex = np.frexp(amax / 6.0)
        byte = np.where(mant > 0.5, ex, ex - 1) + 127
    byte = np.clip(np.where(amax > 0, byte, 1), 1, 254)
    scaled = (w * np.exp2(127.0 - byte)[:, None, :]).reshape(k, n).astype(np.float32)
    by_word = np.ascontiguousarray(scaled.reshape(k // 512, 128, 4, n).transpose(0, 1, 3, 2))
    if fmt == "e4m3":
        words = by_word.astype(ml_dtypes.float8_e4m3fn).view(np.uint8)
    else:
        c = by_word.astype(ml_dtypes.float4_e2m1fn).view(np.uint8) & 0xF
        words = c[..., 0::2] | (c[..., 1::2] << 4)
    return np.ascontiguousarray(words), np.ascontiguousarray(byte.astype(np.uint8).reshape(k // 512, 16, n))


def unpack_weight(words, scales, fmt):
    g, p, n, _ = words.shape
    if fmt == "e4m3":
        vals = np.ascontiguousarray(words).view(ml_dtypes.float8_e4m3fn).astype(np.float64)
    else:
        nib = np.empty((g, p, n, 4), np.uint8)
        nib[..., 0::2] = words & 0xF
        nib[..., 1::2] = words >> 4
        vals = E2M1[nib]
    vals = vals * np.repeat(np.exp2(scales.astype(np.float64) - 127.0), 8, axis=1)[..., None]
    return vals.transpose(0, 1, 3, 2).reshape(g * 512, n)


N, D, C, R = 512, 1024, 1280, 5120
SCALE = 20.0
FMT = "e4m3"


def softplus(v):
    return np.logaddexp(v, 0.0)


def inv_softplus(y):
    return y + np.log(-np.expm1(-y))


def setup_inputs():
    s = mx_kscale(D)
    x = np.random.standard_normal((N, D)) * (0.6 + 0.8 * np.random.random_sample((N, 1)))
    var = (2.0 / D) * np.exp(np.random.standard_normal((C, D)) + 0.5 * np.random.standard_normal((C, 1)))
    cls_w = np.random.standard_normal((C, D)) * 0.15 / np.sqrt(D) / s
    cls_b = bf(np.random.standard_normal(C) * 0.3)
    bbox_w = np.random.standard_normal((R, D)) / np.sqrt(D) / s
    bbox_b = bf(np.random.standard_normal(R) * 0.3)
    cls_w_words, cls_w_scales = pack_weight(np.ascontiguousarray(cls_w.T), FMT)
    bbox_w_words, bbox_w_scales = pack_weight(np.ascontiguousarray(bbox_w.T), FMT)
    return {"x": bf(x * s),
            "cls_w_words": cls_w_words,
            "cls_w_scales": cls_w_scales,
            "cls_b": cls_b,
            "sigma_w": bf(inv_softplus(var / (s * s))),
            "bbox_w_words": bbox_w_words,
            "bbox_w_scales": bbox_w_scales,
            "bbox_b": bbox_b}


def reference(x, cls_w_words, cls_w_scales, cls_b, sigma_w, bbox_w_words, bbox_w_scales, bbox_b):
    x = f64(x)
    var = softplus(f64(sigma_w))
    xq = mxq(x, 1, "e4m3")
    m = xq @ unpack_weight(cls_w_words, cls_w_scales, FMT)
    v = mxq(x * x, 1, "e4m3") @ mxq(var, 1, "e4m3").T
    k = 1.0 / np.sqrt(1.0 + (np.pi / 8.0) * v)
    scores = SCALE * k * m + f64(cls_b)[None, :]
    proposal_deltas = (xq @ unpack_weight(bbox_w_words, bbox_w_scales, FMT)) + f64(bbox_b)[None, :]
    return scores, proposal_deltas

@@ -1,0 +1,262 @@
+from contextlib import ExitStack
+import math
+
+import concourse.mybir as mybir
+from concourse.masks import make_identity
+
+FP8X4 = mybir.dt.float8_e4m3fn_x4
+BF16 = mybir.dt.bfloat16
+F32 = mybir.dt.float32
+I32 = mybir.dt.int32
+U32 = mybir.dt.uint32
+U8 = mybir.dt.uint8
+ACT = mybir.ActivationFunctionType
+ALU = mybir.AluOpType
+
+P = 128
+TOKENS, D, C, R = 512, 1024, 1280, 5120
+K_PASS = 4 * P
+PASSES = D // K_PASS
+WORDS = K_PASS // 2
+TOKEN_TILES = TOKENS // P
+BANK = 512
+C_PAIR = 2 * P
+C_PAIRS = C // C_PAIR
+R_CHUNK = 2 * BANK
+R_CHUNKS = R // R_CHUNK
+SIGN_BITS = -2147450880
+ROUND_TO_STEP = 1.5
+PAIRS_PER_GROUP = 2
+
+FLOPS = 2 * TOKENS * D * (C + C + R)
+
+
+def tile_bayesianoutputlayers_kernel(
+    tc, x, cls_w_words, cls_w_scales, cls_b, sigma_w, bbox_w_words, bbox_w_scales, bbox_b, out_0, out_1
+):
+    nc = tc.nc
+    with ExitStack() as stack:
+        keep = stack.enter_context(tc.tile_pool(name="keep", bufs=1))
+        loads = stack.enter_context(tc.tile_pool(name="loads", bufs=2))
+        stage = stack.enter_context(tc.tile_pool(name="stage", bufs=4))
+        work = stack.enter_context(tc.tile_pool(name="work", bufs=2))
+        delta_out = stack.enter_context(tc.tile_pool(name="delta_out", bufs=3))
+        score_out = stack.enter_context(tc.tile_pool(name="score_out", bufs=3))
+        delta_banks = stack.enter_context(tc.psum_pool(name="delta_banks", bufs=4))
+        other_banks = stack.enter_context(tc.psum_pool(name="other_banks", bufs=4))
+
+        x_sb = keep.tile([P, TOKEN_TILES, D], BF16)
+        nc.sync.dma_start(out=x_sb[:], in_=x.rearrange("(r p) k -> p r k", p=P))
+
+        identity = keep.tile([P, P], F32)
+        make_identity(nc, identity[:])
+
+        bbox_planes = keep.tile([P, R], U8, align_bytes=64)
+        cls_planes = keep.tile([P, C], U8, align_bytes=64)
+        nc.vector.memset(bbox_planes[:].bitcast(I32), 0)
+        nc.vector.memset(cls_planes[:].bitcast(I32), 0)
+
+        def load_planes(planes, scales):
+            for quadrant in range(4):
+                nc.sync.dma_start(
+                    out=planes[32 * quadrant : 32 * quadrant + 4 * PASSES, :].bitcast(I32),
+                    in_=scales[:, 4 * quadrant : 4 * quadrant + 4, :].bitcast(I32),
+                )
+
+        load_planes(bbox_planes, bbox_w_scales)
+
+        bbox_bias = keep.tile([P, R], BF16)
+        cls_bias = keep.tile([P, C], BF16)
+        for j in range(R_CHUNKS):
+            chunk = slice(R_CHUNK * j, R_CHUNK * (j + 1))
+            nc.scalar.dma_start(out=bbox_bias[:, chunk], in_=bbox_b[chunk].partition_broadcast(P))
+        nc.scalar.dma_start(out=cls_bias[:], in_=cls_b.partition_broadcast(P))
+
+        x_words = x_sb[:].bitcast(F32)
+        x_codes = keep.tile([P, PASSES, TOKENS], U32, align_bytes=64)
+        x_scales = keep.tile([P, PASSES, TOKENS], U8, align_bytes=64)
+        xx_codes = keep.tile([P, PASSES, TOKENS], U32, align_bytes=64)
+        xx_scales = keep.tile([P, PASSES, TOKENS], U8, align_bytes=64)
+        for g in range(PASSES):
+            x_grouped = stage.tile([P, TOKENS, 2], F32, tag="stage", align_bytes=64)
+            xx_grouped = stage.tile([P, 4 * TOKENS], BF16, tag="stage", align_bytes=64)
+            for side in range(2):
+                flipped = other_banks.tile([P, 2, 2 * P], F32, tag="bank")
+                for u in range(2):
+                    for i in range(2):
+                        nc.tensor.transpose(
+                            flipped[:, u, i * P : (i + 1) * P],
+                            x_words[:, 2 * side + i, WORDS * g + u : WORDS * (g + 1) : 2],
+                            identity[:],
+                        )
+                tokens = slice(2 * P * side, 2 * P * (side + 1))
+                nc.scalar.copy(out=x_grouped[:, tokens, :], in_=flipped[:].rearrange("p u c -> p c u"))
+            x_values = x_grouped[:].rearrange("p c u -> p (c u)").bitcast(BF16)
+            nc.vector.quantize_mx(out=x_codes[:, g, :].bitcast(FP8X4), scales=x_scales[:, g, :], in_=x_values)
+            nc.gpsimd.tensor_tensor(out=xx_grouped[:], in0=x_values, in1=x_values, op=ALU.mult)
+            nc.vector.quantize_mx(out=xx_codes[:, g, :].bitcast(FP8X4), scales=xx_scales[:, g, :], in_=xx_grouped[:])
+
+        def deltas_chunk(j):
+            bbox_words = loads.tile([P, PASSES, R_CHUNK], U32, align_bytes=64)
+            nc.sync.dma_start(
+                out=bbox_words[:].bitcast(I32),
+                in_=bbox_w_words[:, :, R_CHUNK * j : R_CHUNK * (j + 1), :]
+                .rearrange("g p n t -> p g (n t)")
+                .bitcast(I32),
+            )
+            for r in range(TOKEN_TILES):
+                deltas = delta_out.tile([P, R_CHUNK], F32)
+                for side in range(2):
+                    first = R_CHUNK * j + BANK * side
+                    acc = delta_banks.tile([P, BANK], F32)
+                    for g in range(PASSES):
+                        nc.tensor.matmul_mx(
+                            out=acc[:],
+                            lhsT=x_codes[:, g, P * r : P * (r + 1)].bitcast(FP8X4),
+                            lhsT_scale=x_scales[:, g, P * r : P * (r + 1)],
+                            rhs=bbox_words[:, g, BANK * side : BANK * (side + 1)].bitcast(FP8X4),
+                            rhs_scale=bbox_planes[4 * g : P, first : first + BANK],
+                            start=(g == 0),
+                            stop=(g == PASSES - 1),
+                        )
+                    nc.vector.tensor_tensor(
+                        out=deltas[:, BANK * side : BANK * (side + 1)],
+                        in0=acc[:],
+                        in1=bbox_bias[:, first : first + BANK],
+                        op=ALU.add,
+                    )
+                nc.sync.dma_start(
+                    out=out_1[P * r : P * (r + 1), R_CHUNK * j : R_CHUNK * (j + 1)], in_=deltas[:]
+                )
+
+        w_grouped = keep.tile([P, PASSES, C, 2], F32)
+        odds_all = keep.tile([P, C_PAIRS, PASSES, 4 * C_PAIR], F32)
+        mid_all = keep.tile([P, C_PAIRS, PASSES, 4 * C_PAIR], F32)
+
+        def w_pair(j):
+            return w_grouped[:, :, C_PAIR * j : C_PAIR * (j + 1), :].rearrange("p g c u -> p g (c u)")
+
+        def sigmoids_of_pair(j):
+            sigma_sb = loads.tile([P, 2, D], BF16)
+            nc.sync.dma_start(
+                out=sigma_sb[:],
+                in_=sigma_w[C_PAIR * j : C_PAIR * (j + 1), :].rearrange("(i p) k -> p i k", p=P),
+            )
+            sigma_words = sigma_sb[:].bitcast(F32)
+            for i in range(2):
+                flipped = other_banks.tile([P, PASSES, 2, P], F32, tag="bank")
+                for g in range(PASSES):
+                    for u in range(2):
+                        nc.tensor.transpose(
+                            flipped[:, g, u, :],
+                            sigma_words[:, i, WORDS * g + u : WORDS * (g + 1) : 2],
+                            identity[:],
+                        )
+                first = C_PAIR * j + P * i
+                nc.scalar.copy(
+                    out=w_grouped[:, :, first : first + P, :],
+                    in_=flipped[:].rearrange("p g u c -> p g c u"),
+                )
+            minus_abs = stage.tile([P, PASSES, 4 * C_PAIR], BF16, tag="stage", align_bytes=64)
+            nc.vector.tensor_scalar(
+                out=minus_abs[:].bitcast(I32),
+                in0=w_pair(j).bitcast(I32),
+                scalar1=SIGN_BITS,
+                scalar2=None,
+                op0=ALU.bitwise_or,
+            )
+            nc.scalar.activation(out=odds_all[:, j], in_=minus_abs[:], func=ACT.Sigmoid)
+            nc.scalar.activation(out=mid_all[:, j], in_=minus_abs[:], func=ACT.Sigmoid, bias=-math.log(2.0))
+
+        var_codes = keep.tile([P, PASSES, C], U32, align_bytes=64)
+        var_scales = keep.tile([P, PASSES, C], U8, align_bytes=64)
+
+        def log_of_pair(j):
+            nc.scalar.activation(out=odds_all[:, j], in_=odds_all[:, j], func=ACT.Ln, scale=-1.0, bias=1.0)
+
+        def var_of_pair(j):
+            gap = odds_all[:, j]
+            mid = mid_all[:, j]
+            nc.vector.scalar_tensor_tensor(out=gap, in0=gap, scalar=0.5, in1=mid, op0=ALU.mult, op1=ALU.add)
+            nc.vector.tensor_scalar(
+                out=gap, in0=gap, scalar1=ROUND_TO_STEP, scalar2=ROUND_TO_STEP, op0=ALU.add, op1=ALU.subtract
+            )
+            nc.gpsimd.tensor_tensor(out=gap, in0=mid, in1=gap, op=ALU.subtract)
+            w_positive = stage.tile([P, PASSES, 4 * C_PAIR], BF16, tag="stage", align_bytes=64)
+            nc.vector.tensor_scalar(
+                out=w_positive[:], in0=w_pair(j).bitcast(BF16), scalar1=0.0, scalar2=None, op0=ALU.max
+            )
+            var_grouped = stage.tile([P, PASSES, 4 * C_PAIR], BF16, tag="stage", align_bytes=64)
+            nc.vector.scalar_tensor_tensor(
+                out=var_grouped[:], in0=gap, scalar=2.0, in1=w_positive[:], op0=ALU.mult, op1=ALU.add
+            )
+            for g in range(PASSES):
+                nc.vector.quantize_mx(
+                    out=var_codes[:, g, C_PAIR * j : C_PAIR * (j + 1)].bitcast(FP8X4),
+                    scales=var_scales[:, g, C_PAIR * j : C_PAIR * (j + 1)],
+                    in_=var_grouped[:, g, :],
+                )
+
+        cls_words = keep.tile([P, PASSES, C], U32, align_bytes=64)
+
+        def scores_chunk(first, width):
+            cols = slice(first, first + width)
+            for r in range(TOKEN_TILES):
+                rows = slice(P * r, P * (r + 1))
+                m_acc = other_banks.tile([P, BANK], F32, tag="bank")
+                v_acc = other_banks.tile([P, BANK], F32, tag="bank")
+                for g in range(PASSES):
+                    nc.tensor.matmul_mx(
+                        out=m_acc[:, :width],
+                        lhsT=x_codes[:, g, rows].bitcast(FP8X4),
+                        lhsT_scale=x_scales[:, g, rows],
+                        rhs=cls_words[:, g, cols].bitcast(FP8X4),
+                        rhs_scale=cls_planes[4 * g : P, cols],
+                        start=(g == 0),
+                        stop=(g == PASSES - 1),
+                    )
+                for g in range(PASSES):
+                    nc.tensor.matmul_mx(
+                        out=v_acc[:, :width],
+                        lhsT=xx_codes[:, g, rows].bitcast(FP8X4),
+                        lhsT_scale=xx_scales[:, g, rows],
+                        rhs=var_codes[:, g, cols].bitcast(FP8X4),
+                        rhs_scale=var_scales[:, g, cols],
+                        start=(g == 0),
+                        stop=(g == PASSES - 1),
+                    )
+                factor = work.tile([P, BANK], F32)
+                nc.scalar.activation(
+                    out=factor[:, :width],
+                    in_=v_acc[:, :width],
+                    func=ACT.Abs_reciprocal_sqrt,
+                    scale=math.pi / 3200.0,
+                    bias=1.0 / 400.0,
+                )
+                scores = score_out.tile([P, BANK], F32)
+                nc.vector.tensor_tensor(out=scores[:, :width], in0=m_acc[:, :width], in1=factor[:, :width], op=ALU.mult)
+                nc.gpsimd.tensor_tensor(out=scores[:, :width], in0=scores[:, :width], in1=cls_bias[:, cols], op=ALU.add)
+                nc.sync.dma_start(out=out_0[rows, cols], in_=scores[:, :width])
+
+        deltas_chunk(0)
+        for first_pair in range(0, C_PAIRS, PAIRS_PER_GROUP):
+            group = range(first_pair, min(first_pair + PAIRS_PER_GROUP, C_PAIRS))
+            for j in group:
+                sigmoids_of_pair(j)
+            for j in group:
+                log_of_pair(j)
+            deltas_chunk(1 + first_pair // PAIRS_PER_GROUP)
+        load_planes(cls_planes, cls_w_scales)
+        nc.sync.dma_start(
+            out=cls_words[:].bitcast(I32),
+            in_=cls_w_words.rearrange("g p n t -> p g (n t)").bitcast(I32),
+        )
+        scored = 0
+        for j in range(C_PAIRS):
+            var_of_pair(j)
+            if j == 0:
+                deltas_chunk(R_CHUNKS - 1)
+            ready = C_PAIR * (j + 1)
+            if ready - scored >= BANK or ready == C:
+                scores_chunk(scored, ready - scored)
+                scored = ready

@@ -65,12 +65,26 @@ def tile_bayesianoutputlayers_kernel(
 
         load_planes(bbox_planes, bbox_w_scales)
 
-        bbox_bias = keep.tile([P, R], BF16)
-        cls_bias = keep.tile([P, C], BF16)
-        for j in range(R_CHUNKS):
-            chunk = slice(R_CHUNK * j, R_CHUNK * (j + 1))
-            nc.scalar.dma_start(out=bbox_bias[:, chunk], in_=bbox_b[chunk].partition_broadcast(P))
-        nc.scalar.dma_start(out=cls_bias[:], in_=cls_b.partition_broadcast(P))
+        bias_rows = keep.tile([P, R + C], BF16)
+        nc.vector.memset(bias_rows[:].bitcast(I32), 0)
+        nc.sync.dma_start(out=bias_rows[0:1, :R], in_=bbox_b.unsqueeze(0))
+        nc.sync.dma_start(out=bias_rows[0:1, R:], in_=cls_b.unsqueeze(0))
+        ones = keep.tile([P, P], BF16)
+        nc.vector.memset(ones[:], 1.0)
+        bias = keep.tile([P, R + C], BF16)
+        for first in range(0, R + C, 2 * BANK):
+            width = min(2 * BANK, R + C - first)
+            spread = other_banks.tile([P, 2 * BANK], BF16, tag="bank")
+            for start in range(0, width, BANK):
+                stop = min(start + BANK, width)
+                nc.tensor.matmul(
+                    out=spread[:, start:stop],
+                    lhsT=ones[:],
+                    rhs=bias_rows[:, first + start : first + stop],
+                    start=True,
+                    stop=True,
+                )
+            nc.scalar.copy(out=bias[:, first : first + width], in_=spread[:, :width])
 
         x_words = x_sb[:].bitcast(F32)
         x_codes = keep.tile([P, PASSES, TOKENS], U32, align_bytes=64)
@@ -79,7 +93,7 @@ def tile_bayesianoutputlayers_kernel(
         xx_scales = keep.tile([P, PASSES, TOKENS], U8, align_bytes=64)
         for g in range(PASSES):
             x_grouped = stage.tile([P, TOKENS, 2], F32, tag="stage", align_bytes=64)
-            xx_grouped = stage.tile([P, 4 * TOKENS], BF16, tag="stage", align_bytes=64)
+            xx_grouped = stage.tile([P, TOKENS, 2, 2], BF16, tag="stage", align_bytes=64)
             for side in range(2):
                 flipped = other_banks.tile([P, 2, 2 * P], F32, tag="bank")
                 for u in range(2):
@@ -91,10 +105,21 @@ def tile_bayesianoutputlayers_kernel(
                         )
                 tokens = slice(2 * P * side, 2 * P * (side + 1))
                 nc.scalar.copy(out=x_grouped[:, tokens, :], in_=flipped[:].rearrange("p u c -> p c u"))
-            x_values = x_grouped[:].rearrange("p c u -> p (c u)").bitcast(BF16)
-            nc.vector.quantize_mx(out=x_codes[:, g, :].bitcast(FP8X4), scales=x_scales[:, g, :], in_=x_values)
-            nc.gpsimd.tensor_tensor(out=xx_grouped[:], in0=x_values, in1=x_values, op=ALU.mult)
-            nc.vector.quantize_mx(out=xx_codes[:, g, :].bitcast(FP8X4), scales=xx_scales[:, g, :], in_=xx_grouped[:])
+                nc.scalar.activation(
+                    out=xx_grouped[:, tokens, :, :],
+                    in_=flipped[:].bitcast(BF16).rearrange("p u (c e) -> p c u e", e=2),
+                    func=ACT.Square,
+                )
+            nc.vector.quantize_mx(
+                out=x_codes[:, g, :].bitcast(FP8X4),
+                scales=x_scales[:, g, :],
+                in_=x_grouped[:].rearrange("p c u -> p (c u)").bitcast(BF16),
+            )
+            nc.vector.quantize_mx(
+                out=xx_codes[:, g, :].bitcast(FP8X4),
+                scales=xx_scales[:, g, :],
+                in_=xx_grouped[:].rearrange("p c u e -> p (c u e)"),
+            )
 
         def deltas_chunk(j):
             bbox_words = loads.tile([P, PASSES, R_CHUNK], U32, align_bytes=64)
@@ -122,7 +147,7 @@ def tile_bayesianoutputlayers_kernel(
                     nc.vector.tensor_tensor(
                         out=deltas[:, BANK * side : BANK * (side + 1)],
                         in0=acc[:],
-                        in1=bbox_bias[:, first : first + BANK],
+                        in1=bias[:, first : first + BANK],
                         op=ALU.add,
                     )
                 nc.sync.dma_start(
@@ -181,7 +206,7 @@ def tile_bayesianoutputlayers_kernel(
             nc.vector.tensor_scalar(
                 out=gap, in0=gap, scalar1=ROUND_TO_STEP, scalar2=ROUND_TO_STEP, op0=ALU.add, op1=ALU.subtract
             )
-            nc.gpsimd.tensor_tensor(out=gap, in0=mid, in1=gap, op=ALU.subtract)
+            nc.vector.tensor_tensor(out=gap, in0=mid, in1=gap, op=ALU.subtract)
             w_positive = stage.tile([P, PASSES, 4 * C_PAIR], BF16, tag="stage", align_bytes=64)
             nc.vector.tensor_scalar(
                 out=w_positive[:], in0=w_pair(j).bitcast(BF16), scalar1=0.0, scalar2=None, op0=ALU.max
@@ -235,7 +260,9 @@ def tile_bayesianoutputlayers_kernel(
                 )
                 scores = score_out.tile([P, BANK], F32)
                 nc.vector.tensor_tensor(out=scores[:, :width], in0=m_acc[:, :width], in1=factor[:, :width], op=ALU.mult)
-                nc.gpsimd.tensor_tensor(out=scores[:, :width], in0=scores[:, :width], in1=cls_bias[:, cols], op=ALU.add)
+                nc.vector.tensor_tensor(
+                    out=scores[:, :width], in0=scores[:, :width], in1=bias[:, R + first : R + first + width], op=ALU.add
+                )
                 nc.sync.dma_start(out=out_0[rows, cols], in_=scores[:, :width])
 
         deltas_chunk(0)

@@ -206,7 +206,7 @@ def tile_bayesianoutputlayers_kernel(
             nc.vector.tensor_scalar(
                 out=gap, in0=gap, scalar1=ROUND_TO_STEP, scalar2=ROUND_TO_STEP, op0=ALU.add, op1=ALU.subtract
             )
-            nc.vector.tensor_tensor(out=gap, in0=mid, in1=gap, op=ALU.subtract)
+            nc.gpsimd.tensor_tensor(out=gap, in0=mid, in1=gap, op=ALU.subtract)
             w_positive = stage.tile([P, PASSES, 4 * C_PAIR], BF16, tag="stage", align_bytes=64)
             nc.vector.tensor_scalar(
                 out=w_positive[:], in0=w_pair(j).bitcast(BF16), scalar1=0.0, scalar2=None, op0=ALU.max
@@ -260,7 +260,7 @@ def tile_bayesianoutputlayers_kernel(
                 )
                 scores = score_out.tile([P, BANK], F32)
                 nc.vector.tensor_tensor(out=scores[:, :width], in0=m_acc[:, :width], in1=factor[:, :width], op=ALU.mult)
-                nc.vector.tensor_tensor(
+                nc.gpsimd.tensor_tensor(
                     out=scores[:, :width], in0=scores[:, :width], in1=bias[:, R + first : R + first + width], op=ALU.add
                 )
                 nc.sync.dma_start(out=out_0[rows, cols], in_=scores[:, :width])

@@ -24,9 +24,9 @@ C_PAIR = 2 * P
 C_PAIRS = C // C_PAIR
 R_CHUNK = 2 * BANK
 R_CHUNKS = R // R_CHUNK
-SIGN_BITS = -2147450880
-ROUND_TO_STEP = 1.5
-PAIRS_PER_GROUP = 2
+ROUND_TO_STEP = 3.0
+AWAY_FLOOR = 2.0**-60
+GROUP = 2
 
 FLOPS = 2 * TOKENS * D * (C + C + R)
 
@@ -38,10 +38,10 @@ def tile_bayesianoutputlayers_kernel(
     with ExitStack() as stack:
         keep = stack.enter_context(tc.tile_pool(name="keep", bufs=1))
         loads = stack.enter_context(tc.tile_pool(name="loads", bufs=2))
-        stage = stack.enter_context(tc.tile_pool(name="stage", bufs=4))
+        stage = stack.enter_context(tc.tile_pool(name="stage", bufs=3))
         work = stack.enter_context(tc.tile_pool(name="work", bufs=2))
         delta_out = stack.enter_context(tc.tile_pool(name="delta_out", bufs=3))
-        score_out = stack.enter_context(tc.tile_pool(name="score_out", bufs=3))
+        score_out = stack.enter_context(tc.tile_pool(name="score_out", bufs=2))
         delta_banks = stack.enter_context(tc.psum_pool(name="delta_banks", bufs=4))
         other_banks = stack.enter_context(tc.psum_pool(name="other_banks", bufs=4))
 
@@ -50,6 +50,13 @@ def tile_bayesianoutputlayers_kernel(
 
         identity = keep.tile([P, P], F32)
         make_identity(nc, identity[:])
+
+        bias_rows = keep.tile([P, R + C], BF16)
+        nc.vector.memset(bias_rows[:].bitcast(I32), 0)
+        nc.scalar.dma_start(out=bias_rows[0:1, :R], in_=bbox_b.unsqueeze(0))
+        nc.scalar.dma_start(out=bias_rows[0:1, R:], in_=cls_b.unsqueeze(0))
+        ones = keep.tile([P, P], BF16)
+        nc.vector.memset(ones[:], 1.0)
 
         bbox_planes = keep.tile([P, R], U8, align_bytes=64)
         cls_planes = keep.tile([P, C], U8, align_bytes=64)
@@ -65,35 +72,13 @@ def tile_bayesianoutputlayers_kernel(
 
         load_planes(bbox_planes, bbox_w_scales)
 
-        bias_rows = keep.tile([P, R + C], BF16)
-        nc.vector.memset(bias_rows[:].bitcast(I32), 0)
-        nc.sync.dma_start(out=bias_rows[0:1, :R], in_=bbox_b.unsqueeze(0))
-        nc.sync.dma_start(out=bias_rows[0:1, R:], in_=cls_b.unsqueeze(0))
-        ones = keep.tile([P, P], BF16)
-        nc.vector.memset(ones[:], 1.0)
-        bias = keep.tile([P, R + C], BF16)
-        for first in range(0, R + C, 2 * BANK):
-            width = min(2 * BANK, R + C - first)
-            spread = other_banks.tile([P, 2 * BANK], BF16, tag="bank")
-            for start in range(0, width, BANK):
-                stop = min(start + BANK, width)
-                nc.tensor.matmul(
-                    out=spread[:, start:stop],
-                    lhsT=ones[:],
-                    rhs=bias_rows[:, first + start : first + stop],
-                    start=True,
-                    stop=True,
-                )
-            nc.scalar.copy(out=bias[:, first : first + width], in_=spread[:, :width])
-
         x_words = x_sb[:].bitcast(F32)
         x_codes = keep.tile([P, PASSES, TOKENS], U32, align_bytes=64)
         x_scales = keep.tile([P, PASSES, TOKENS], U8, align_bytes=64)
         xx_codes = keep.tile([P, PASSES, TOKENS], U32, align_bytes=64)
         xx_scales = keep.tile([P, PASSES, TOKENS], U8, align_bytes=64)
+        x_grouped = keep.tile([P, PASSES, 2 * TOKENS], F32, align_bytes=64)
         for g in range(PASSES):
-            x_grouped = stage.tile([P, TOKENS, 2], F32, tag="stage", align_bytes=64)
-            xx_grouped = stage.tile([P, TOKENS, 2, 2], BF16, tag="stage", align_bytes=64)
             for side in range(2):
                 flipped = other_banks.tile([P, 2, 2 * P], F32, tag="bank")
                 for u in range(2):
@@ -103,23 +88,36 @@ def tile_bayesianoutputlayers_kernel(
                             x_words[:, 2 * side + i, WORDS * g + u : WORDS * (g + 1) : 2],
                             identity[:],
                         )
-                tokens = slice(2 * P * side, 2 * P * (side + 1))
-                nc.scalar.copy(out=x_grouped[:, tokens, :], in_=flipped[:].rearrange("p u c -> p c u"))
-                nc.scalar.activation(
-                    out=xx_grouped[:, tokens, :, :],
-                    in_=flipped[:].bitcast(BF16).rearrange("p u (c e) -> p c u e", e=2),
-                    func=ACT.Square,
+                nc.scalar.copy(
+                    out=x_grouped[:, g, 4 * P * side : 4 * P * (side + 1)].rearrange("p (c u) -> p c u", u=2),
+                    in_=flipped[:].rearrange("p u c -> p c u"),
                 )
             nc.vector.quantize_mx(
-                out=x_codes[:, g, :].bitcast(FP8X4),
-                scales=x_scales[:, g, :],
-                in_=x_grouped[:].rearrange("p c u -> p (c u)").bitcast(BF16),
+                out=x_codes[:, g, :].bitcast(FP8X4), scales=x_scales[:, g, :], in_=x_grouped[:, g, :].bitcast(BF16)
             )
-            nc.vector.quantize_mx(
-                out=xx_codes[:, g, :].bitcast(FP8X4),
-                scales=xx_scales[:, g, :],
-                in_=xx_grouped[:].rearrange("p c u e -> p (c u e)"),
-            )
+
+        bias = keep.tile([P, R + C], BF16)
+        for first in range(0, R + C, 2 * BANK):
+            width = min(2 * BANK, R + C - first)
+            spread = delta_banks.tile([P, 2 * BANK], BF16, tag="bank")
+            for start in range(0, width, BANK):
+                stop = min(start + BANK, width)
+                nc.tensor.matmul(
+                    out=spread[:, start:stop],
+                    lhsT=ones[:],
+                    rhs=bias_rows[:, first + start : first + stop],
+                    start=True,
+                    stop=True,
+                )
+            nc.vector.tensor_copy(out=bias[:, first : first + width], in_=spread[:, :width])
+
+        def square_x():
+            for g in range(PASSES):
+                xx_grouped = stage.tile([P, 4 * TOKENS], BF16, tag="stage", align_bytes=64)
+                nc.scalar.activation(out=xx_grouped[:], in_=x_grouped[:, g, :].bitcast(BF16), func=ACT.Square)
+                nc.vector.quantize_mx(
+                    out=xx_codes[:, g, :].bitcast(FP8X4), scales=xx_scales[:, g, :], in_=xx_grouped[:]
+                )
 
         def deltas_chunk(j):
             bbox_words = loads.tile([P, PASSES, R_CHUNK], U32, align_bytes=64)
@@ -133,7 +131,7 @@ def tile_bayesianoutputlayers_kernel(
                 deltas = delta_out.tile([P, R_CHUNK], F32)
                 for side in range(2):
                     first = R_CHUNK * j + BANK * side
-                    acc = delta_banks.tile([P, BANK], F32)
+                    acc = delta_banks.tile([P, BANK], F32, tag="bank")
                     for g in range(PASSES):
                         nc.tensor.matmul_mx(
                             out=acc[:],
@@ -155,7 +153,7 @@ def tile_bayesianoutputlayers_kernel(
                 )
 
         w_grouped = keep.tile([P, PASSES, C, 2], F32)
-        odds_all = keep.tile([P, C_PAIRS, PASSES, 4 * C_PAIR], F32)
+        away_all = keep.tile([P, C_PAIRS, PASSES, 4 * C_PAIR], F32)
         mid_all = keep.tile([P, C_PAIRS, PASSES, 4 * C_PAIR], F32)
 
         def w_pair(j):
@@ -182,39 +180,27 @@ def tile_bayesianoutputlayers_kernel(
                     out=w_grouped[:, :, first : first + P, :],
                     in_=flipped[:].rearrange("p g u c -> p g c u"),
                 )
-            minus_abs = stage.tile([P, PASSES, 4 * C_PAIR], BF16, tag="stage", align_bytes=64)
-            nc.vector.tensor_scalar(
-                out=minus_abs[:].bitcast(I32),
-                in0=w_pair(j).bitcast(I32),
-                scalar1=SIGN_BITS,
-                scalar2=None,
-                op0=ALU.bitwise_or,
-            )
-            nc.scalar.activation(out=odds_all[:, j], in_=minus_abs[:], func=ACT.Sigmoid)
-            nc.scalar.activation(out=mid_all[:, j], in_=minus_abs[:], func=ACT.Sigmoid, bias=-math.log(2.0))
+            w_values = w_pair(j).bitcast(BF16)
+            nc.scalar.activation(out=away_all[:, j], in_=w_values, func=ACT.Sigmoid, scale=-1.0)
+            nc.scalar.activation(out=mid_all[:, j], in_=w_values, func=ACT.Sigmoid, bias=-math.log(2.0))
 
         var_codes = keep.tile([P, PASSES, C], U32, align_bytes=64)
         var_scales = keep.tile([P, PASSES, C], U8, align_bytes=64)
 
         def log_of_pair(j):
-            nc.scalar.activation(out=odds_all[:, j], in_=odds_all[:, j], func=ACT.Ln, scale=-1.0, bias=1.0)
+            nc.scalar.activation(out=away_all[:, j], in_=away_all[:, j], func=ACT.Ln, bias=AWAY_FLOOR)
 
         def var_of_pair(j):
-            gap = odds_all[:, j]
+            gap = away_all[:, j]
             mid = mid_all[:, j]
-            nc.vector.scalar_tensor_tensor(out=gap, in0=gap, scalar=0.5, in1=mid, op0=ALU.mult, op1=ALU.add)
+            nc.vector.scalar_tensor_tensor(out=gap, in0=mid, scalar=2.0, in1=gap, op0=ALU.mult, op1=ALU.add)
             nc.vector.tensor_scalar(
                 out=gap, in0=gap, scalar1=ROUND_TO_STEP, scalar2=ROUND_TO_STEP, op0=ALU.add, op1=ALU.subtract
             )
-            nc.gpsimd.tensor_tensor(out=gap, in0=mid, in1=gap, op=ALU.subtract)
-            w_positive = stage.tile([P, PASSES, 4 * C_PAIR], BF16, tag="stage", align_bytes=64)
-            nc.vector.tensor_scalar(
-                out=w_positive[:], in0=w_pair(j).bitcast(BF16), scalar1=0.0, scalar2=None, op0=ALU.max
-            )
+            bounded = stage.tile([P, PASSES, 4 * C_PAIR], BF16, tag="stage", align_bytes=64)
+            nc.vector.scalar_tensor_tensor(out=bounded[:], in0=mid, scalar=2.0, in1=gap, op0=ALU.mult, op1=ALU.subtract)
             var_grouped = stage.tile([P, PASSES, 4 * C_PAIR], BF16, tag="stage", align_bytes=64)
-            nc.vector.scalar_tensor_tensor(
-                out=var_grouped[:], in0=gap, scalar=2.0, in1=w_positive[:], op0=ALU.mult, op1=ALU.add
-            )
+            nc.vector.tensor_tensor(out=var_grouped[:], in0=bounded[:], in1=w_pair(j).bitcast(BF16), op=ALU.max)
             for g in range(PASSES):
                 nc.vector.quantize_mx(
                     out=var_codes[:, g, C_PAIR * j : C_PAIR * (j + 1)].bitcast(FP8X4),
@@ -260,19 +246,20 @@ def tile_bayesianoutputlayers_kernel(
                 )
                 scores = score_out.tile([P, BANK], F32)
                 nc.vector.tensor_tensor(out=scores[:, :width], in0=m_acc[:, :width], in1=factor[:, :width], op=ALU.mult)
-                nc.gpsimd.tensor_tensor(
+                nc.vector.tensor_tensor(
                     out=scores[:, :width], in0=scores[:, :width], in1=bias[:, R + first : R + first + width], op=ALU.add
                 )
                 nc.sync.dma_start(out=out_0[rows, cols], in_=scores[:, :width])
 
+        groups = [range(0, 1)] + [range(j, min(j + GROUP, C_PAIRS)) for j in range(1, C_PAIRS, GROUP)]
         deltas_chunk(0)
-        for first_pair in range(0, C_PAIRS, PAIRS_PER_GROUP):
-            group = range(first_pair, min(first_pair + PAIRS_PER_GROUP, C_PAIRS))
-            for j in group:
+        for n in range(len(groups)):
+            for j in groups[n]:
                 sigmoids_of_pair(j)
-            for j in group:
+            for j in groups[n]:
                 log_of_pair(j)
-            deltas_chunk(1 + first_pair // PAIRS_PER_GROUP)
+            deltas_chunk(n + 1)
+        square_x()
         load_planes(cls_planes, cls_w_scales)
         nc.sync.dma_start(
             out=cls_words[:].bitcast(I32),
@@ -281,8 +268,8 @@ def tile_bayesianoutputlayers_kernel(
         scored = 0
         for j in range(C_PAIRS):
             var_of_pair(j)
-            if j == 0:
-                deltas_chunk(R_CHUNKS - 1)
+            if len(groups) + 1 + j < R_CHUNKS:
+                deltas_chunk(len(groups) + 1 + j)
             ready = C_PAIR * (j + 1)
             if ready - scored >= BANK or ready == C:
                 scores_chunk(scored, ready - scored)

@@ -53,8 +53,8 @@ def tile_bayesianoutputlayers_kernel(
 
         bias_rows = keep.tile([P, R + C], BF16)
         nc.vector.memset(bias_rows[:].bitcast(I32), 0)
-        nc.scalar.dma_start(out=bias_rows[0:1, :R], in_=bbox_b.unsqueeze(0))
-        nc.scalar.dma_start(out=bias_rows[0:1, R:], in_=cls_b.unsqueeze(0))
+        nc.sync.dma_start(out=bias_rows[0:1, :R], in_=bbox_b.unsqueeze(0))
+        nc.sync.dma_start(out=bias_rows[0:1, R:], in_=cls_b.unsqueeze(0))
         ones = keep.tile([P, P], BF16)
         nc.vector.memset(ones[:], 1.0)
 
@@ -109,7 +109,7 @@ def tile_bayesianoutputlayers_kernel(
                     start=True,
                     stop=True,
                 )
-            nc.vector.tensor_copy(out=bias[:, first : first + width], in_=spread[:, :width])
+            nc.scalar.copy(out=bias[:, first : first + width], in_=spread[:, :width])
 
         def square_x():
             for g in range(PASSES):

@@ -22,6 +22,7 @@ TOKEN_TILES = TOKENS // P
 BANK = 512
 C_PAIR = 2 * P
 C_PAIRS = C // C_PAIR
+C_TILES = C // P
 R_CHUNK = 2 * BANK
 R_CHUNKS = R // R_CHUNK
 ROUND_TO_STEP = 3.0
@@ -51,12 +52,17 @@ def tile_bayesianoutputlayers_kernel(
         identity = keep.tile([P, P], F32)
         make_identity(nc, identity[:])
 
-        bias_rows = keep.tile([P, R + C], BF16)
-        nc.vector.memset(bias_rows[:].bitcast(I32), 0)
-        nc.sync.dma_start(out=bias_rows[0:1, :R], in_=bbox_b.unsqueeze(0))
-        nc.sync.dma_start(out=bias_rows[0:1, R:], in_=cls_b.unsqueeze(0))
+        bbox_rows = keep.tile([P, R], BF16)
+        nc.vector.memset(bbox_rows[:].bitcast(I32), 0)
+        nc.sync.dma_start(out=bbox_rows[0:1, :], in_=bbox_b.unsqueeze(0))
         ones = keep.tile([P, P], BF16)
         nc.vector.memset(ones[:], 1.0)
+
+        cls_rows = keep.tile([P, P], BF16)
+        nc.vector.memset(cls_rows[:].bitcast(I32), 0)
+        nc.sync.dma_start(out=cls_rows[0:C_TILES, :], in_=cls_b.rearrange("(t p) -> t p", p=P))
+        identity_bf16 = keep.tile([P, P], BF16)
+        make_identity(nc, identity_bf16[:])
 
         bbox_planes = keep.tile([P, R], U8, align_bytes=64)
         cls_planes = keep.tile([P, C], U8, align_bytes=64)
@@ -96,20 +102,22 @@ def tile_bayesianoutputlayers_kernel(
                 out=x_codes[:, g, :].bitcast(FP8X4), scales=x_scales[:, g, :], in_=x_grouped[:, g, :].bitcast(BF16)
             )
 
-        bias = keep.tile([P, R + C], BF16)
-        for first in range(0, R + C, 2 * BANK):
-            width = min(2 * BANK, R + C - first)
+        bbox_bias = keep.tile([P, R], BF16)
+        for first in range(0, R, 2 * BANK):
             spread = delta_banks.tile([P, 2 * BANK], BF16, tag="bank")
-            for start in range(0, width, BANK):
-                stop = min(start + BANK, width)
+            for side in range(2):
                 nc.tensor.matmul(
-                    out=spread[:, start:stop],
+                    out=spread[:, BANK * side : BANK * (side + 1)],
                     lhsT=ones[:],
-                    rhs=bias_rows[:, first + start : first + stop],
+                    rhs=bbox_rows[:, first + BANK * side : first + BANK * (side + 1)],
                     start=True,
                     stop=True,
                 )
-            nc.scalar.copy(out=bias[:, first : first + width], in_=spread[:, :width])
+            nc.vector.tensor_copy(out=bbox_bias[:, first : first + 2 * BANK], in_=spread[:])
+        cls_bias = keep.tile([P, C_TILES], F32)
+        cls_flipped = other_banks.tile([P, P], BF16, tag="bank")
+        nc.tensor.transpose(cls_flipped[:], cls_rows[:], identity_bf16[:])
+        nc.vector.tensor_copy(out=cls_bias[:], in_=cls_flipped[:, :C_TILES])
 
         def square_x():
             for g in range(PASSES):
@@ -145,7 +153,7 @@ def tile_bayesianoutputlayers_kernel(
                     nc.vector.tensor_tensor(
                         out=deltas[:, BANK * side : BANK * (side + 1)],
                         in0=acc[:],
-                        in1=bias[:, first : first + BANK],
+                        in1=bbox_bias[:, first : first + BANK],
                         op=ALU.add,
                     )
                 nc.sync.dma_start(
@@ -210,46 +218,47 @@ def tile_bayesianoutputlayers_kernel(
 
         cls_words = keep.tile([P, PASSES, C], U32, align_bytes=64)
 
-        def scores_chunk(first, width):
-            cols = slice(first, first + width)
+        def scores_tile(t):
+            cols = slice(P * t, P * (t + 1))
+            m_acc = other_banks.tile([P, TOKENS], F32, tag="bank")
+            v_acc = other_banks.tile([P, TOKENS], F32, tag="bank")
+            for g in range(PASSES):
+                nc.tensor.matmul_mx(
+                    out=m_acc[:],
+                    lhsT=cls_words[:, g, cols].bitcast(FP8X4),
+                    lhsT_scale=cls_planes[4 * g : P, cols],
+                    rhs=x_codes[:, g, :].bitcast(FP8X4),
+                    rhs_scale=x_scales[:, g, :],
+                    start=(g == 0),
+                    stop=(g == PASSES - 1),
+                )
+            for g in range(PASSES):
+                nc.tensor.matmul_mx(
+                    out=v_acc[:],
+                    lhsT=var_codes[:, g, cols].bitcast(FP8X4),
+                    lhsT_scale=var_scales[:, g, cols],
+                    rhs=xx_codes[:, g, :].bitcast(FP8X4),
+                    rhs_scale=xx_scales[:, g, :],
+                    start=(g == 0),
+                    stop=(g == PASSES - 1),
+                )
+            factor = work.tile([P, TOKENS], F32)
+            nc.scalar.activation(
+                out=factor[:],
+                in_=v_acc[:],
+                func=ACT.Abs_reciprocal_sqrt,
+                scale=math.pi / 3200.0,
+                bias=1.0 / 400.0,
+            )
+            by_column = work.tile([P, TOKENS], F32)
+            nc.vector.tensor_tensor(out=by_column[:], in0=m_acc[:], in1=factor[:], op=ALU.mult)
+            nc.scalar.activation(out=by_column[:], in_=by_column[:], func=ACT.Identity, bias=cls_bias[:, t : t + 1])
+            by_token = delta_banks.tile([P, TOKEN_TILES, P], F32, tag="bank")
             for r in range(TOKEN_TILES):
-                rows = slice(P * r, P * (r + 1))
-                m_acc = other_banks.tile([P, BANK], F32, tag="bank")
-                v_acc = other_banks.tile([P, BANK], F32, tag="bank")
-                for g in range(PASSES):
-                    nc.tensor.matmul_mx(
-                        out=m_acc[:, :width],
-                        lhsT=x_codes[:, g, rows].bitcast(FP8X4),
-                        lhsT_scale=x_scales[:, g, rows],
-                        rhs=cls_words[:, g, cols].bitcast(FP8X4),
-                        rhs_scale=cls_planes[4 * g : P, cols],
-                        start=(g == 0),
-                        stop=(g == PASSES - 1),
-                    )
-                for g in range(PASSES):
-                    nc.tensor.matmul_mx(
-                        out=v_acc[:, :width],
-                        lhsT=xx_codes[:, g, rows].bitcast(FP8X4),
-                        lhsT_scale=xx_scales[:, g, rows],
-                        rhs=var_codes[:, g, cols].bitcast(FP8X4),
-                        rhs_scale=var_scales[:, g, cols],
-                        start=(g == 0),
-                        stop=(g == PASSES - 1),
-                    )
-                factor = work.tile([P, BANK], F32)
-                nc.scalar.activation(
-                    out=factor[:, :width],
-                    in_=v_acc[:, :width],
-                    func=ACT.Abs_reciprocal_sqrt,
-                    scale=math.pi / 3200.0,
-                    bias=1.0 / 400.0,
-                )
-                scores = score_out.tile([P, BANK], F32)
-                nc.vector.tensor_tensor(out=scores[:, :width], in0=m_acc[:, :width], in1=factor[:, :width], op=ALU.mult)
-                nc.vector.tensor_tensor(
-                    out=scores[:, :width], in0=scores[:, :width], in1=bias[:, R + first : R + first + width], op=ALU.add
-                )
-                nc.sync.dma_start(out=out_0[rows, cols], in_=scores[:, :width])
+                nc.tensor.transpose(by_token[:, r, :], by_column[:, P * r : P * (r + 1)], identity[:])
+            scores = score_out.tile([P, TOKEN_TILES, P], F32)
+            nc.scalar.copy(out=scores[:], in_=by_token[:])
+            nc.sync.dma_start(out=out_0[:, cols].rearrange("(r p) c -> p r c", p=P), in_=scores[:])
 
         groups = [range(0, 1)] + [range(j, min(j + GROUP, C_PAIRS)) for j in range(1, C_PAIRS, GROUP)]
         deltas_chunk(0)
@@ -265,12 +274,9 @@ def tile_bayesianoutputlayers_kernel(
             out=cls_words[:].bitcast(I32),
             in_=cls_w_words.rearrange("g p n t -> p g (n t)").bitcast(I32),
         )
-        scored = 0
         for j in range(C_PAIRS):
             var_of_pair(j)
             if len(groups) + 1 + j < R_CHUNKS:
                 deltas_chunk(len(groups) + 1 + j)
-            ready = C_PAIR * (j + 1)
-            if ready - scored >= BANK or ready == C:
-                scores_chunk(scored, ready - scored)
-                scored = ready
+            scores_tile(2 * j)
+            scores_tile(2 * j + 1)

@@ -49,6 +49,11 @@ def tile_bayesianoutputlayers_kernel(
         x_sb = keep.tile([P, TOKEN_TILES, D], BF16)
         nc.sync.dma_start(out=x_sb[:], in_=x.rearrange("(r p) k -> p r k", p=P))
 
+        tiny = keep.tile([P, 1], F32)
+        warm = keep.tile([P, 1], F32)
+        nc.vector.memset(tiny[:], 0.0)
+        nc.scalar.activation(out=warm[:], in_=tiny[:], func=ACT.Sigmoid)
+
         identity = keep.tile([P, P], F32)
         make_identity(nc, identity[:])
 

@@ -28,6 +28,7 @@ R_CHUNKS = R // R_CHUNK
 ROUND_TO_STEP = 3.0
 AWAY_FLOOR = 2.0**-60
 GROUP = 2
+LAST_ON_VECTOR = 4
 
 FLOPS = 2 * TOKENS * D * (C + C + R)
 
@@ -47,7 +48,8 @@ def tile_bayesianoutputlayers_kernel(
         other_banks = stack.enter_context(tc.psum_pool(name="other_banks", bufs=4))
 
         x_sb = keep.tile([P, TOKEN_TILES, D], BF16)
-        nc.sync.dma_start(out=x_sb[:], in_=x.rearrange("(r p) k -> p r k", p=P))
+        for r in range(TOKEN_TILES):
+            nc.sync.dma_start(out=x_sb[:, r, :], in_=x[P * r : P * (r + 1), :])
 
         tiny = keep.tile([P, 1], F32)
         warm = keep.tile([P, 1], F32)
@@ -89,8 +91,8 @@ def tile_bayesianoutputlayers_kernel(
         xx_codes = keep.tile([P, PASSES, TOKENS], U32, align_bytes=64)
         xx_scales = keep.tile([P, PASSES, TOKENS], U8, align_bytes=64)
         x_grouped = keep.tile([P, PASSES, 2 * TOKENS], F32, align_bytes=64)
-        for g in range(PASSES):
-            for side in range(2):
+        for side in range(2):
+            for g in range(PASSES):
                 flipped = other_banks.tile([P, 2, 2 * P], F32, tag="bank")
                 for u in range(2):
                     for i in range(2):
@@ -103,9 +105,11 @@ def tile_bayesianoutputlayers_kernel(
                     out=x_grouped[:, g, 4 * P * side : 4 * P * (side + 1)].rearrange("p (c u) -> p c u", u=2),
                     in_=flipped[:].rearrange("p u c -> p c u"),
                 )
-            nc.vector.quantize_mx(
-                out=x_codes[:, g, :].bitcast(FP8X4), scales=x_scales[:, g, :], in_=x_grouped[:, g, :].bitcast(BF16)
-            )
+                nc.vector.quantize_mx(
+                    out=x_codes[:, g, 2 * P * side : 2 * P * (side + 1)].bitcast(FP8X4),
+                    scales=x_scales[:, g, 2 * P * side : 2 * P * (side + 1)],
+                    in_=x_grouped[:, g, 4 * P * side : 4 * P * (side + 1)].bitcast(BF16),
+                )
 
         bbox_bias = keep.tile([P, R], BF16)
         for first in range(0, R, 2 * BANK):
@@ -257,7 +261,12 @@ def tile_bayesianoutputlayers_kernel(
             )
             by_column = work.tile([P, TOKENS], F32)
             nc.vector.tensor_tensor(out=by_column[:], in0=m_acc[:], in1=factor[:], op=ALU.mult)
-            nc.scalar.activation(out=by_column[:], in_=by_column[:], func=ACT.Identity, bias=cls_bias[:, t : t + 1])
+            if t < C_TILES - LAST_ON_VECTOR:
+                nc.scalar.activation(out=by_column[:], in_=by_column[:], func=ACT.Identity, bias=cls_bias[:, t : t + 1])
+            else:
+                nc.vector.tensor_scalar(
+                    out=by_column[:], in0=by_column[:], scalar1=cls_bias[:, t : t + 1], scalar2=None, op0=ALU.add
+                )
             by_token = delta_banks.tile([P, TOKEN_TILES, P], F32, tag="bank")
             for r in range(TOKEN_TILES):
                 nc.tensor.transpose(by_token[:, r, :], by_column[:, P * r : P * (r + 1)], identity[:])

@@ -274,14 +274,15 @@ def tile_bayesianoutputlayers_kernel(
             nc.scalar.copy(out=scores[:], in_=by_token[:])
             nc.sync.dma_start(out=out_0[:, cols].rearrange("(r p) c -> p r c", p=P), in_=scores[:])
 
-        groups = [range(0, 1)] + [range(j, min(j + GROUP, C_PAIRS)) for j in range(1, C_PAIRS, GROUP)]
+        groups = [range(0, 1), range(1, 2), range(2, 3), range(3, C_PAIRS)]
         deltas_chunk(0)
-        for n in range(len(groups)):
-            for j in groups[n]:
-                sigmoids_of_pair(j)
-            for j in groups[n]:
-                log_of_pair(j)
-            deltas_chunk(n + 1)
+        with tc.manual_schedule(engines={mybir.EngineType.Activation}):
+            for n in range(len(groups)):
+                for j in groups[n]:
+                    sigmoids_of_pair(j)
+                for j in groups[n]:
+                    log_of_pair(j)
+                deltas_chunk(n + 1)
         square_x()
         load_planes(cls_planes, cls_w_scales)
         nc.sync.dma_start(

from contextlib import ExitStack
import math

import concourse.mybir as mybir
from concourse.masks import make_identity

FP8X4 = mybir.dt.float8_e4m3fn_x4
BF16 = mybir.dt.bfloat16
F32 = mybir.dt.float32
I32 = mybir.dt.int32
U32 = mybir.dt.uint32
U8 = mybir.dt.uint8
ACT = mybir.ActivationFunctionType
ALU = mybir.AluOpType

P = 128
TOKENS, D, C, R = 512, 1024, 1280, 5120
K_PASS = 4 * P
PASSES = D // K_PASS
WORDS = K_PASS // 2
TOKEN_TILES = TOKENS // P
BANK = 512
C_PAIR = 2 * P
C_PAIRS = C // C_PAIR
C_TILES = C // P
R_CHUNK = 2 * BANK
R_CHUNKS = R // R_CHUNK
ROUND_TO_STEP = 3.0
AWAY_FLOOR = 2.0**-60
GROUP = 2
LAST_ON_VECTOR = 4

FLOPS = 2 * TOKENS * D * (C + C + R)


def tile_bayesianoutputlayers_kernel(
    tc, x, cls_w_words, cls_w_scales, cls_b, sigma_w, bbox_w_words, bbox_w_scales, bbox_b, out_0, out_1
):
    nc = tc.nc
    with ExitStack() as stack:
        keep = stack.enter_context(tc.tile_pool(name="keep", bufs=1))
        loads = stack.enter_context(tc.tile_pool(name="loads", bufs=2))
        stage = stack.enter_context(tc.tile_pool(name="stage", bufs=3))
        work = stack.enter_context(tc.tile_pool(name="work", bufs=2))
        delta_out = stack.enter_context(tc.tile_pool(name="delta_out", bufs=3))
        score_out = stack.enter_context(tc.tile_pool(name="score_out", bufs=2))
        delta_banks = stack.enter_context(tc.psum_pool(name="delta_banks", bufs=4))
        other_banks = stack.enter_context(tc.psum_pool(name="other_banks", bufs=4))

        x_sb = keep.tile([P, TOKEN_TILES, D], BF16)
        for r in range(TOKEN_TILES):
            nc.sync.dma_start(out=x_sb[:, r, :], in_=x[P * r : P * (r + 1), :])

        tiny = keep.tile([P, 1], F32)
        warm = keep.tile([P, 1], F32)
        nc.vector.memset(tiny[:], 0.0)
        nc.scalar.activation(out=warm[:], in_=tiny[:], func=ACT.Sigmoid)

        identity = keep.tile([P, P], F32)
        make_identity(nc, identity[:])

        bbox_rows = keep.tile([P, R], BF16)
        nc.vector.memset(bbox_rows[:].bitcast(I32), 0)
        nc.sync.dma_start(out=bbox_rows[0:1, :], in_=bbox_b.unsqueeze(0))
        ones = keep.tile([P, P], BF16)
        nc.vector.memset(ones[:], 1.0)

        cls_rows = keep.tile([P, P], BF16)
        nc.vector.memset(cls_rows[:].bitcast(I32), 0)
        nc.sync.dma_start(out=cls_rows[0:C_TILES, :], in_=cls_b.rearrange("(t p) -> t p", p=P))
        identity_bf16 = keep.tile([P, P], BF16)
        make_identity(nc, identity_bf16[:])

        bbox_planes = keep.tile([P, R], U8, align_bytes=64)
        cls_planes = keep.tile([P, C], U8, align_bytes=64)
        nc.vector.memset(bbox_planes[:].bitcast(I32), 0)
        nc.vector.memset(cls_planes[:].bitcast(I32), 0)

        def load_planes(planes, scales):
            for quadrant in range(4):
                nc.sync.dma_start(
                    out=planes[32 * quadrant : 32 * quadrant + 4 * PASSES, :].bitcast(I32),
                    in_=scales[:, 4 * quadrant : 4 * quadrant + 4, :].bitcast(I32),
                )

        load_planes(bbox_planes, bbox_w_scales)

        x_words = x_sb[:].bitcast(F32)
        x_codes = keep.tile([P, PASSES, TOKENS], U32, align_bytes=64)
        x_scales = keep.tile([P, PASSES, TOKENS], U8, align_bytes=64)
        xx_codes = keep.tile([P, PASSES, TOKENS], U32, align_bytes=64)
        xx_scales = keep.tile([P, PASSES, TOKENS], U8, align_bytes=64)
        x_grouped = keep.tile([P, PASSES, 2 * TOKENS], F32, align_bytes=64)
        for side in range(2):
            for g in range(PASSES):
                flipped = other_banks.tile([P, 2, 2 * P], F32, tag="bank")
                for u in range(2):
                    for i in range(2):
                        nc.tensor.transpose(
                            flipped[:, u, i * P : (i + 1) * P],
                            x_words[:, 2 * side + i, WORDS * g + u : WORDS * (g + 1) : 2],
                            identity[:],
                        )
                nc.scalar.copy(
                    out=x_grouped[:, g, 4 * P * side : 4 * P * (side + 1)].rearrange("p (c u) -> p c u", u=2),
                    in_=flipped[:].rearrange("p u c -> p c u"),
                )
                nc.vector.quantize_mx(
                    out=x_codes[:, g, 2 * P * side : 2 * P * (side + 1)].bitcast(FP8X4),
                    scales=x_scales[:, g, 2 * P * side : 2 * P * (side + 1)],
                    in_=x_grouped[:, g, 4 * P * side : 4 * P * (side + 1)].bitcast(BF16),
                )

        bbox_bias = keep.tile([P, R], BF16)
        for first in range(0, R, 2 * BANK):
            spread = delta_banks.tile([P, 2 * BANK], BF16, tag="bank")
            for side in range(2):
                nc.tensor.matmul(
                    out=spread[:, BANK * side : BANK * (side + 1)],
                    lhsT=ones[:],
                    rhs=bbox_rows[:, first + BANK * side : first + BANK * (side + 1)],
                    start=True,
                    stop=True,
                )
            nc.vector.tensor_copy(out=bbox_bias[:, first : first + 2 * BANK], in_=spread[:])
        cls_bias = keep.tile([P, C_TILES], F32)
        cls_flipped = other_banks.tile([P, P], BF16, tag="bank")
        nc.tensor.transpose(cls_flipped[:], cls_rows[:], identity_bf16[:])
        nc.vector.tensor_copy(out=cls_bias[:], in_=cls_flipped[:, :C_TILES])

        def square_x():
            for g in range(PASSES):
                xx_grouped = stage.tile([P, 4 * TOKENS], BF16, tag="stage", align_bytes=64)
                nc.scalar.activation(out=xx_grouped[:], in_=x_grouped[:, g, :].bitcast(BF16), func=ACT.Square)
                nc.vector.quantize_mx(
                    out=xx_codes[:, g, :].bitcast(FP8X4), scales=xx_scales[:, g, :], in_=xx_grouped[:]
                )

        def deltas_chunk(j):
            bbox_words = loads.tile([P, PASSES, R_CHUNK], U32, align_bytes=64)
            nc.sync.dma_start(
                out=bbox_words[:].bitcast(I32),
                in_=bbox_w_words[:, :, R_CHUNK * j : R_CHUNK * (j + 1), :]
                .rearrange("g p n t -> p g (n t)")
                .bitcast(I32),
            )
            for r in range(TOKEN_TILES):
                deltas = delta_out.tile([P, R_CHUNK], F32)
                for side in range(2):
                    first = R_CHUNK * j + BANK * side
                    acc = delta_banks.tile([P, BANK], F32, tag="bank")
                    for g in range(PASSES):
                        nc.tensor.matmul_mx(
                            out=acc[:],
                            lhsT=x_codes[:, g, P * r : P * (r + 1)].bitcast(FP8X4),
                            lhsT_scale=x_scales[:, g, P * r : P * (r + 1)],
                            rhs=bbox_words[:, g, BANK * side : BANK * (side + 1)].bitcast(FP8X4),
                            rhs_scale=bbox_planes[4 * g : P, first : first + BANK],
                            start=(g == 0),
                            stop=(g == PASSES - 1),
                        )
                    nc.vector.tensor_tensor(
                        out=deltas[:, BANK * side : BANK * (side + 1)],
                        in0=acc[:],
                        in1=bbox_bias[:, first : first + BANK],
                        op=ALU.add,
                    )
                nc.sync.dma_start(
                    out=out_1[P * r : P * (r + 1), R_CHUNK * j : R_CHUNK * (j + 1)], in_=deltas[:]
                )

        w_grouped = keep.tile([P, PASSES, C, 2], F32)
        away_all = keep.tile([P, C_PAIRS, PASSES, 4 * C_PAIR], F32)
        mid_all = keep.tile([P, C_PAIRS, PASSES, 4 * C_PAIR], F32)

        def w_pair(j):
            return w_grouped[:, :, C_PAIR * j : C_PAIR * (j + 1), :].rearrange("p g c u -> p g (c u)")

        def sigmoids_of_pair(j):
            sigma_sb = loads.tile([P, 2, D], BF16)
            nc.sync.dma_start(
                out=sigma_sb[:],
                in_=sigma_w[C_PAIR * j : C_PAIR * (j + 1), :].rearrange("(i p) k -> p i k", p=P),
            )
            sigma_words = sigma_sb[:].bitcast(F32)
            for i in range(2):
                flipped = other_banks.tile([P, PASSES, 2, P], F32, tag="bank")
                for g in range(PASSES):
                    for u in range(2):
                        nc.tensor.transpose(
                            flipped[:, g, u, :],
                            sigma_words[:, i, WORDS * g + u : WORDS * (g + 1) : 2],
                            identity[:],
                        )
                first = C_PAIR * j + P * i
                nc.scalar.copy(
                    out=w_grouped[:, :, first : first + P, :],
                    in_=flipped[:].rearrange("p g u c -> p g c u"),
                )
            w_values = w_pair(j).bitcast(BF16)
            nc.scalar.activation(out=away_all[:, j], in_=w_values, func=ACT.Sigmoid, scale=-1.0)
            nc.scalar.activation(out=mid_all[:, j], in_=w_values, func=ACT.Sigmoid, bias=-math.log(2.0))

        var_codes = keep.tile([P, PASSES, C], U32, align_bytes=64)
        var_scales = keep.tile([P, PASSES, C], U8, align_bytes=64)

        def log_of_pair(j):
            nc.scalar.activation(out=away_all[:, j], in_=away_all[:, j], func=ACT.Ln, bias=AWAY_FLOOR)

        def var_of_pair(j):
            gap = away_all[:, j]
            mid = mid_all[:, j]
            nc.vector.scalar_tensor_tensor(out=gap, in0=mid, scalar=2.0, in1=gap, op0=ALU.mult, op1=ALU.add)
            nc.vector.tensor_scalar(
                out=gap, in0=gap, scalar1=ROUND_TO_STEP, scalar2=ROUND_TO_STEP, op0=ALU.add, op1=ALU.subtract
            )
            bounded = stage.tile([P, PASSES, 4 * C_PAIR], BF16, tag="stage", align_bytes=64)
            nc.vector.scalar_tensor_tensor(out=bounded[:], in0=mid, scalar=2.0, in1=gap, op0=ALU.mult, op1=ALU.subtract)
            var_grouped = stage.tile([P, PASSES, 4 * C_PAIR], BF16, tag="stage", align_bytes=64)
            nc.vector.tensor_tensor(out=var_grouped[:], in0=bounded[:], in1=w_pair(j).bitcast(BF16), op=ALU.max)
            for g in range(PASSES):
                nc.vector.quantize_mx(
                    out=var_codes[:, g, C_PAIR * j : C_PAIR * (j + 1)].bitcast(FP8X4),
                    scales=var_scales[:, g, C_PAIR * j : C_PAIR * (j + 1)],
                    in_=var_grouped[:, g, :],
                )

        cls_words = keep.tile([P, PASSES, C], U32, align_bytes=64)

        def scores_tile(t):
            cols = slice(P * t, P * (t + 1))
            m_acc = other_banks.tile([P, TOKENS], F32, tag="bank")
            v_acc = other_banks.tile([P, TOKENS], F32, tag="bank")
            for g in range(PASSES):
                nc.tensor.matmul_mx(
                    out=m_acc[:],
                    lhsT=cls_words[:, g, cols].bitcast(FP8X4),
                    lhsT_scale=cls_planes[4 * g : P, cols],
                    rhs=x_codes[:, g, :].bitcast(FP8X4),
                    rhs_scale=x_scales[:, g, :],
                    start=(g == 0),
                    stop=(g == PASSES - 1),
                )
            for g in range(PASSES):
                nc.tensor.matmul_mx(
                    out=v_acc[:],
                    lhsT=var_codes[:, g, cols].bitcast(FP8X4),
                    lhsT_scale=var_scales[:, g, cols],
                    rhs=xx_codes[:, g, :].bitcast(FP8X4),
                    rhs_scale=xx_scales[:, g, :],
                    start=(g == 0),
                    stop=(g == PASSES - 1),
                )
            factor = work.tile([P, TOKENS], F32)
            nc.scalar.activation(
                out=factor[:],
                in_=v_acc[:],
                func=ACT.Abs_reciprocal_sqrt,
                scale=math.pi / 3200.0,
                bias=1.0 / 400.0,
            )
            by_column = work.tile([P, TOKENS], F32)
            nc.vector.tensor_tensor(out=by_column[:], in0=m_acc[:], in1=factor[:], op=ALU.mult)
            if t < C_TILES - LAST_ON_VECTOR:
                nc.scalar.activation(out=by_column[:], in_=by_column[:], func=ACT.Identity, bias=cls_bias[:, t : t + 1])
            else:
                nc.vector.tensor_scalar(
                    out=by_column[:], in0=by_column[:], scalar1=cls_bias[:, t : t + 1], scalar2=None, op0=ALU.add
                )
            by_token = delta_banks.tile([P, TOKEN_TILES, P], F32, tag="bank")
            for r in range(TOKEN_TILES):
                nc.tensor.transpose(by_token[:, r, :], by_column[:, P * r : P * (r + 1)], identity[:])
            scores = score_out.tile([P, TOKEN_TILES, P], F32)
            nc.scalar.copy(out=scores[:], in_=by_token[:])
            nc.sync.dma_start(out=out_0[:, cols].rearrange("(r p) c -> p r c", p=P), in_=scores[:])

        groups = [range(0, 1), range(1, 2), range(2, 3), range(3, C_PAIRS)]
        deltas_chunk(0)
        with tc.manual_schedule(engines={mybir.EngineType.Activation}):
            for n in range(len(groups)):
                for j in groups[n]:
                    sigmoids_of_pair(j)
                for j in groups[n]:
                    log_of_pair(j)
                deltas_chunk(n + 1)
        square_x()
        load_planes(cls_planes, cls_w_scales)
        nc.sync.dma_start(
            out=cls_words[:].bitcast(I32),
            in_=cls_w_words.rearrange("g p n t -> p g (n t)").bitcast(I32),
        )
        for j in range(C_PAIRS):
            var_of_pair(j)
            if len(groups) + 1 + j < R_CHUNKS:
                deltas_chunk(len(groups) + 1 + j)
            scores_tile(2 * j)
            scores_tile(2 * j + 1)
